import numpy as np
import ml_dtypes


def mxq(x, axis, fmt="e4m3"):
    dtype, down = {"e4m3": (ml_dtypes.float8_e4m3fn, 7), "e5m2": (ml_dtypes.float8_e5m2, 14)}[fmt]
    v = np.moveaxis(np.asarray(x, np.float32).astype(ml_dtypes.bfloat16).astype(np.float64), axis, -1)
    blocks = v.reshape(v.shape[:-1] + (-1, 32))
    amax = np.abs(blocks).max(-1, keepdims=True)
    byte = np.maximum(np.where(amax > 0, np.frexp(amax)[1] - 1 + 127, 0) - down, 1)
    scale = np.exp2(byte - 127.0)
    codes = (blocks / scale).astype(np.float32).astype(dtype).astype(np.float64)
    return np.moveaxis((codes * scale).reshape(v.shape), -1, axis)


WIDE = False


def mx_kscale(k):
    if not WIDE:
        return np.ones(k)
    levels = np.array([10, -10, 5, -5, 0])
    if k % 512:
        return np.exp2(np.random.permutation(np.resize(levels, k // 32))).repeat(32)
    a = np.empty((k // 512, 16))
    for p in range(k // 512):
        a[p, :8] = np.random.permutation(np.resize(levels, 8))
        for g in range(8):
            far = levels[np.abs(levels - a[p, g]) >= 10]
            a[p, g + 8] = far[np.random.randint(len(far))]
    return np.exp2(a.ravel()).repeat(32)


BF16 = ml_dtypes.bfloat16


def bf(x):
    return np.asarray(x, np.float32).astype(BF16)


def f64(x):
    return np.asarray(x).astype(np.float64)


B, IN, H, OUT, L, STEPS = 1024, 512, 1024, 128, 3, 3
LN_EPS = 1e-5
TAU_EPS = 1e-6


def layer_norm(v, g, b):
    m = v.mean(-1, keepdims=True)
    var = ((v - m) ** 2).mean(-1, keepdims=True)
    return (v - m) / np.sqrt(var + LN_EPS) * g + b


def draw0():
    r = mx_kscale(IN)
    s = mx_kscale(H)
    s = s / s.max()
    t = mx_kscale(H)
    liq_rms = np.sqrt(L * (L + 1) / 2.0)
    return {"liq": bf(np.random.standard_normal((B, H)) * liq_rms * s),
            "h": bf(np.random.standard_normal((B, H))),
            "x": bf(np.random.standard_normal((B, IN)) * r),
            "W_in": bf(np.random.standard_normal((H, IN)) * 0.7 / np.sqrt(IN) / r),
            "b_in": bf(np.random.standard_normal(H) * 0.3),
            "W_v": bf(np.random.standard_normal((H, H)) / np.sqrt(H) * t[:, None] / s),
            "b_v": bf(np.random.standard_normal(H) * 0.5 * t),
            "W_o": bf(np.random.standard_normal((H, H)) / np.sqrt(H) / t),
            "b_o": bf(np.random.standard_normal(H) * 0.5),
            "g_att": bf(1.0 + 0.1 * np.random.standard_normal(H)),
            "beta_att": bf(np.random.standard_normal(H) * 0.3),
            "tau": bf(0.5 + 0.5 * np.random.random(H))}


def core(liq, h, x, W_in, b_in, W_v, b_v, W_o, b_o, g_att, beta_att, tau):
    liq, h = f64(liq), f64(h)
    xin = (mxq(f64(x), 1, "e4m3") @ mxq(f64(W_in), 1, "e4m3").T) + f64(b_in)
    v = (mxq(liq, 1, "e4m3") @ mxq(f64(W_v), 1, "e4m3").T) + f64(b_v)
    att = (mxq(v, 1, "e4m3") @ mxq(f64(W_o), 1, "e4m3").T) + f64(b_o)
    z = layer_norm(att + liq, f64(g_att), f64(beta_att))
    dh = (-h + np.tanh(z + xin)) / (f64(tau) + TAU_EPS)
    return h + dh


def e4m3fn_bytes(y):
    return np.clip(np.asarray(y, np.float64), -448.0, 448.0).astype(np.float32).astype(ml_dtypes.float8_e4m3fn).view(np.uint8)


def e4m3fn_values(b):
    return np.asarray(b, np.uint8).view(ml_dtypes.float8_e4m3fn).astype(np.float64)


def setup_inputs():
    d = draw0()
    x0 = np.asarray(d['W_o']).astype(np.float64)
    s = (np.max(np.abs(x0), axis=(0,), keepdims=True) / 448.0).astype(np.float32)
    out = {}
    for k, v in d.items():
        if k == 'W_o':
            out['W_o_bytes'] = e4m3fn_bytes(x0 / s.astype(np.float64))
            out['W_o_scale'] = s
        else:
            out[k] = v
    return out


def reference(liq, h, x, W_in, b_in, W_v, b_v, W_o_bytes, W_o_scale, b_o, g_att, beta_att, tau):
    return core(liq, h, x, W_in, b_in, W_v, b_v, e4m3fn_values(W_o_bytes) * W_o_scale.astype(np.float64), b_o, g_att, beta_att, tau)

@@ -1,0 +1,516 @@
+from contextlib import ExitStack
+
+import concourse.mybir as mybir
+from concourse.masks import make_identity
+
+B, IN, H = 1024, 512, 1024
+P = 128
+FLOPS = 2 * B * H * (IN + H + H)
+
+F32 = mybir.dt.float32
+BF16 = mybir.dt.bfloat16
+U32 = mybir.dt.uint32
+U8 = mybir.dt.uint8
+FP8 = mybir.dt.float8_e4m3fn
+FP8X4 = mybir.dt.float8_e4m3fn_x4
+
+ALU = mybir.AluOpType
+ACT = mybir.ActivationFunctionType
+
+LN_EPS = 1e-5
+CAST = "GGGGGGGG"
+WROUTE = ["s","p","s","p","s","p","s","p","s","p","s","p","s","p","s","p"]
+SLOTS = [["par","bo","p0","v4","w0"],["p1","w1"],["p5","p3","p7","w2"],["p4","v1","v2","l4","w3"],["v6","p2","l1","p6","w4"],["l0","om","w5"],["x30","v7","w6"],["v5","v0","w7","v3","l2"],["x21","x20V"],["x31","x01"],["l3","x11"],["x10"],["x00"],["l6","l5","l7"]]
+STEP = [["NT",4,1],["G",4,1],["LQ",0,None],["LB",0,None],["VM",0,None],["N",3,0],["T",5,1],["SQ",2,None],["T",4,0],["ST",2,None],["HB",4,None],["F",5,0],["N",3,1],["AM",1,None],["VE",0,None],["A",1,None],["NT",3,0],["VQ",0,None],["G",3,0],["WT",5,1],["F",5,1],["WT",4,0]]
+LOADS = ["o0","p0","v4","p1","o1","p5","p3","p7","p4","v1","v2","l4","o2","v6","p2","l1","p6","l0","o3","v7","v5","v0","v3","l2","l3","l6","l5","l7"]
+TAU_EPS = 1e-6
+
+
+def tile_advancedliquidneuralnetwork_pb_kernel(
+    tc, liq, h, x, W_in, b_in, W_v, b_v, W_o_bytes, W_o_scale, b_o, g_att, beta_att, tau, out
+):
+    nc = tc.nc
+    with ExitStack() as ctx:
+        keep = ctx.enter_context(tc.tile_pool(name="keep", bufs=1))
+        work = ctx.enter_context(tc.tile_pool(name="work", bufs=1))
+        psum = ctx.enter_context(tc.psum_pool(name="psum", bufs=1))
+        ctx.enter_context(tc.manual_schedule())
+
+        def bank(n):
+            return psum.tile([P, 512], F32, name="bank%d" % n, tag="bank%d" % n, bufs=1)
+
+        ident = keep.tile([P, P], F32, name="ident")
+        rows = keep.tile([P, P], BF16, name="rows")
+        rows_f = keep.tile([P, P], F32, name="rows_f")
+        cols = keep.tile([P, 40], F32, name="cols")
+        c_col = keep.tile([P, 8], F32, name="c_col")
+        it_col = keep.tile([P, 8], F32, name="it_col")
+        om_col = keep.tile([P, 8], F32, name="om_col")
+        bv_col = keep.tile([P, 2, 4], BF16, name="bv_col")
+        sc_col = keep.tile([P, 2, 2, 2], F32, name="sc_col")
+        bo_bc = keep.tile([P, H], F32, name="bo_bc")
+        om_bc = keep.tile([P, H], F32, name="om_bc")
+        half_neg = keep.tile([P, 1], F32, name="half_neg")
+        ident_bf = keep.tile([P, P], BF16, name="ident_bf")
+        bo_col = keep.tile([P, 8], BF16, name="bo_col")
+        diag = keep.tile([P, 8, P], F32, name="diag")
+        warm = keep.tile([P, 1], F32, name="warm")
+
+        liq_sb = keep.tile([P, 8, H], BF16, name="liq_sb", align_bytes=64)
+        x_sb = keep.tile([P, 4, 2, IN], BF16, name="x_sb", align_bytes=64)
+        win_sb = keep.tile([P, 4, 2, IN], BF16, name="win_sb", align_bytes=64)
+        wo_sb = keep.tile([P, 8, H], U8, name="wo_sb", align_bytes=64)
+
+        wv_codes = keep.tile([P, 8, 256], U32, name="wv_codes", align_bytes=64)
+        wv_scales = keep.tile([P, 8, 256], U8, name="wv_scales", align_bytes=64)
+        liq_codes = keep.tile([P, 8, 256], U32, name="liq_codes", align_bytes=64)
+        liq_scales = keep.tile([P, 8, 256], U8, name="liq_scales", align_bytes=64)
+        win_codes = keep.tile([P, 4, 256], U32, name="win_codes", align_bytes=64)
+        win_scales = keep.tile([P, 4, 256], U8, name="win_scales", align_bytes=64)
+        x_codes = keep.tile([P, 2, 512], U32, name="x_codes", align_bytes=64)
+        x_scales = keep.tile([P, 2, 512], U8, name="x_scales", align_bytes=64)
+        wo_codes = keep.tile([P, 2, 2, 512], U32, name="wo_codes", align_bytes=64)
+        wo_scales = keep.tile([P, 2, 2, 512], U8, name="wo_scales", align_bytes=64)
+        xs = keep.tile([P, 2, 8, 512], F32, name="xs")
+
+        wv_raw = {}
+        h_raw = {}
+        wv_view = W_v.rearrange("(g m t) k -> g t m k", m=P, t=4)
+        x_view = x.rearrange("(q a p) k -> q p a k", a=2, p=P)
+        win_view = W_in.rearrange("(q a p) k -> q p a k", a=2, p=P)
+        wo_view = W_o_bytes.rearrange("(q a p) k -> q p a k", a=2, p=P)
+        liq_view = liq.rearrange("(i p) k -> i p k", p=P)
+        h_view = h.rearrange("(i p) k -> i p k", p=P)
+        out_view = out.rearrange("(i p) k -> i p k", p=P)
+
+        def load_wv(c):
+            wv_raw[c] = work.tile([P, H], BF16, name="wv_raw", tag="raw", bufs=8, align_bytes=64)
+            nc.sync.dma_start(out=wv_raw[c][:], in_=wv_view[c // 4, c % 4])
+
+        def load_h(i):
+            h_raw[i] = work.tile([P, H], BF16, name="h_raw", tag="raw", bufs=8, align_bytes=64)
+            nc.sync.dma_start(out=h_raw[i][:], in_=h_view[i])
+
+        def load_liq(i):
+            nc.sync.dma_start(out=liq_sb[:, i, :], in_=liq_view[i])
+
+        def load_wo(q):
+            nc.sync.dma_start(out=wo_sb[:, 2 * q : 2 * q + 2, :], in_=wo_view[q])
+
+        def load_pair(e):
+            if e < 4:
+                nc.sync.dma_start(out=win_sb[:, e], in_=win_view[e])
+            else:
+                nc.sync.dma_start(out=x_sb[:, e - 4], in_=x_view[e - 4])
+
+        nc.vector.memset(rows[:], 0.0)
+        nc.vector.memset(half_neg[:], -0.5)
+        nc.vector.memset(warm[:], 0.0)
+        make_identity(nc, ident[:])
+        nc.scalar.dma_start(out=sc_col[:], in_=W_o_scale.rearrange("o (g p u e) -> p (o g) u e", g=2, p=P, u=2))
+        nc.scalar.dma_start(out=bv_col[:], in_=b_v.rearrange("(g p t) -> p g t", g=2, p=P))
+        for n, vec in enumerate((b_in, beta_att, g_att, tau, b_o)):
+            nc.scalar.dma_start(out=rows[8 * n : 8 * n + 8, :], in_=vec.rearrange("(j p) -> j p", p=P))
+        nc.scalar.activation(out=warm[:], in_=warm[:], func=ACT.Tanh)
+
+        loaders = {"o": load_wo, "v": load_wv, "l": load_liq, "p": load_pair}
+        for name in LOADS:
+            loaders[name[0]](int(name[1]))
+
+        rotation = {"order": [2, 3, 4, 5, 6, 7], "at": 0}
+
+        def next_bank():
+            order = rotation["order"]
+            b = bank(order[rotation["at"] % len(order)])
+            rotation["at"] += 1
+            return b
+
+        pending_q = []
+
+        def flush_q(keep_back):
+            while len(pending_q) > keep_back:
+                pending_q.pop(0)()
+
+        def word_transposes(b, words):
+            bv = b[:].rearrange("p (s r) -> p s r", s=4)
+            for s, w in enumerate(words):
+                nc.tensor.transpose(bv[:, s, :], w, ident[:])
+
+        def words_of(tile_ap):
+            w = tile_ap.bitcast(F32)
+            return [w[:, 256 * g + u : 256 * (g + 1) : 2] for g in range(2) for u in range(2)]
+
+        def copy_out(engine, dst_bf16, b):
+            d = dst_bf16.bitcast(F32).rearrange("p (g r u) -> p g r u", g=2, u=2)
+            s = b[:].rearrange("p (g u r) -> p g r u", g=2, u=2)
+            if engine == "v":
+                nc.vector.tensor_copy(out=d, in_=s)
+            else:
+                nc.scalar.copy(out=d, in_=s)
+
+        def quantize(codes, scales, src):
+            nc.vector.quantize_mx(out=codes.bitcast(FP8X4), scales=scales, in_=src)
+
+        def prep_wv(c, engine):
+            b = next_bank()
+            word_transposes(b, words_of(wv_raw[c][:]))
+            gt = work.tile([P, 1024], BF16, name="grouped", tag="grouped", bufs=4, align_bytes=64)
+            copy_out(engine, gt[:], b)
+            pending_q.append(lambda: quantize(wv_codes[:, c, :], wv_scales[:, c, :], gt[:]))
+
+        def prep_liq(i, engine):
+            b = next_bank()
+            word_transposes(b, words_of(liq_sb[:, i, :]))
+            gt = work.tile([P, 1024], BF16, name="grouped", tag="grouped", bufs=4, align_bytes=64)
+            copy_out(engine, gt[:], b)
+            pending_q.append(lambda: quantize(liq_codes[:, i, :], liq_scales[:, i, :], gt[:]))
+
+        x_grouped = {}
+        x_done = []
+
+        def prep_pair(e, engine):
+            b = next_bank()
+            if e < 4:
+                words = [
+                    win_sb[:, e, a, :].bitcast(F32)[:, u:256:2] for a in range(2) for u in range(2)
+                ]
+                gt = work.tile([P, 1024], BF16, name="grouped", tag="grouped", bufs=4, align_bytes=64)
+                word_transposes(b, words)
+                copy_out(engine, gt[:], b)
+                pending_q.append(lambda: quantize(win_codes[:, e, :], win_scales[:, e, :], gt[:]))
+            else:
+                q = e - 4
+                words = [
+                    x_sb[:, q, a, :].bitcast(F32)[:, u:256:2] for a in range(2) for u in range(2)
+                ]
+                if q // 2 not in x_grouped:
+                    x_grouped[q // 2] = work.tile(
+                        [P, 2048], BF16, name="x_grouped", tag="x_grouped", bufs=2, align_bytes=64
+                    )
+                gt = x_grouped[q // 2]
+                word_transposes(b, words)
+                copy_out(engine, gt[:, 1024 * (q % 2) : 1024 * (q % 2) + 1024], b)
+                x_done.append(q)
+                if q ^ 1 in x_done:
+                    pending_q.append(lambda: quantize(x_codes[:, q // 2, :], x_scales[:, q // 2, :], gt[:]))
+
+        wo_bf = {}
+        wo_grouped = {}
+
+        def cast_wo(c):
+            wo_bf[c] = work.tile([P, H], BF16, name="wo_bf", tag="wo_bf", bufs=3, align_bytes=64)
+            src = wo_sb[:, c, :].bitcast(FP8)
+            if CAST[c] == "G":
+                nc.gpsimd.tensor_copy(out=wo_bf[c][:], in_=src)
+            elif CAST[c] == "V":
+                nc.vector.tensor_copy(out=wo_bf[c][:], in_=src)
+            else:
+                nc.scalar.copy(out=wo_bf[c][:], in_=src)
+
+        def prep_wo(c):
+            b = next_bank()
+            word_transposes(b, words_of(wo_bf[c][:]))
+            hf, j = c // 4, c % 4
+            if j == 0:
+                wo_grouped[hf] = work.tile(
+                    [P, 2, 512, 4], BF16, name="wo_grouped", tag="wo_grouped", bufs=2, align_bytes=64
+                )
+            gt = wo_grouped[hf]
+            values = b[:].bitcast(BF16).rearrange("p (g u r e) -> p g r u e", g=2, u=2, e=2)
+            for g in range(2):
+                nc.vector.tensor_tensor(
+                    out=gt[:, g, P * j : P * j + P, :].rearrange("p r (u e) -> p r u e", u=2),
+                    in0=values[:, g],
+                    in1=sc_col[:, g].unsqueeze(1).to_broadcast([P, P, 2, 2]),
+                    op=ALU.mult,
+                )
+            if j == 3:
+                for g in range(2):
+                    pending_q.append(
+                        lambda g=g: quantize(
+                            wo_codes[:, g, hf, :],
+                            wo_scales[:, g, hf, :],
+                            gt[:, g].rearrange("p r t -> p (r t)"),
+                        )
+                    )
+
+        def params():
+            nc.vector.tensor_copy(out=rows_f[:], in_=rows[:])
+            nc.vector.tensor_copy(out=ident_bf[:], in_=ident[:])
+            b = next_bank()
+            nc.tensor.transpose(b[:, 0:P], rows_f[:], ident[:])
+            nc.vector.tensor_copy(out=cols[:], in_=b[:, 0:40])
+            nc.vector.tensor_scalar(
+                out=it_col[:], in0=cols[:, 24:32], scalar1=TAU_EPS, scalar2=None, op0=ALU.add
+            )
+            nc.vector.tensor_tensor(out=c_col[:], in0=cols[:, 0:8], in1=cols[:, 8:16], op=ALU.add)
+            nc.vector.tensor_copy(out=bo_col[:], in_=cols[:, 32:40])
+            nc.vector.reciprocal(out=it_col[:], in_=it_col[:])
+            nc.vector.tensor_scalar(
+                out=om_col[:], in0=it_col[:], scalar1=-1.0, scalar2=1.0, op0=ALU.mult, op1=ALU.add
+            )
+
+        def make_diag():
+            for j in range(8):
+                nc.gpsimd.tensor_scalar(
+                    out=diag[:, j, :], in0=ident[:], scalar1=it_col[:, j : j + 1], scalar2=0.0, op0=ALU.mult, op1=ALU.add
+                )
+
+        def spread(dst, col, eye, halves=(0, 1)):
+            for hf in halves:
+                b = next_bank()
+                for j in range(4):
+                    nc.tensor.matmul(
+                        b[:, P * j : P * j + P],
+                        lhsT=col[:, 4 * hf + j : 4 * hf + j + 1].to_broadcast([P, P]),
+                        rhs=eye[:],
+                        start=True,
+                        stop=True,
+                    )
+                nc.scalar.copy(out=dst[:, 512 * hf : 512 * hf + 512], in_=b[:])
+
+        def xin(j, hf, engine):
+            b = next_bank()
+            nc.tensor.matmul_mx(
+                out=b[:],
+                lhsT=win_codes[:, j // 2, P * (j % 2) : P * (j % 2) + P].bitcast(FP8X4),
+                lhsT_scale=win_scales[:, j // 2, P * (j % 2) : P * (j % 2) + P],
+                rhs=x_codes[:, hf, :].bitcast(FP8X4),
+                rhs_scale=x_scales[:, hf, :],
+                start=True,
+                stop=True,
+            )
+            if engine == "v":
+                nc.vector.tensor_scalar(
+                    out=xs[:, hf, j, :], in0=b[:], scalar1=c_col[:, j : j + 1], scalar2=None, op0=ALU.add
+                )
+            else:
+                nc.scalar.activation(out=xs[:, hf, j, :], in_=b[:], func=ACT.Identity, bias=c_col[:, j : j + 1])
+
+        v_banks, v_grouped, v_codes, v_scales = {}, {}, {}, {}
+
+        def v_matmul(i):
+            v_banks[i] = [bank(0), bank(1)]
+            for go in range(2):
+                for t in range(4):
+                    for kg in range(2):
+                        nc.tensor.matmul_mx(
+                            out=v_banks[i][go][:, P * t : P * t + P],
+                            lhsT=wv_codes[:, 4 * go + t, P * kg : P * kg + P].bitcast(FP8X4),
+                            lhsT_scale=wv_scales[:, 4 * go + t, P * kg : P * kg + P],
+                            rhs=liq_codes[:, i, P * kg : P * kg + P].bitcast(FP8X4),
+                            rhs_scale=liq_scales[:, i, P * kg : P * kg + P],
+                            start=(kg == 0),
+                            stop=(kg == 1),
+                        )
+
+        def v_evac(i):
+            v_grouped[i] = work.tile([P, 2, P, 4], BF16, name="v_grouped", tag="v_grouped", bufs=2, align_bytes=64)
+            for go in range(2):
+                nc.vector.tensor_tensor(
+                    out=v_grouped[i][:, go],
+                    in0=v_banks[i][go][:].rearrange("p (t n) -> p n t", t=4),
+                    in1=bv_col[:, go].unsqueeze(1).to_broadcast([P, P, 4]),
+                    op=ALU.add,
+                )
+
+        def v_quant(i):
+            v_codes[i] = work.tile([P, 256], U32, name="v_codes", tag="v_codes", bufs=2, align_bytes=64)
+            v_scales[i] = work.tile([P, 256], U8, name="v_scales", tag="v_scales", bufs=2, align_bytes=64)
+            quantize(v_codes[i][:], v_scales[i][:], v_grouped[i][:].rearrange("p g n t -> p (g n t)"))
+
+        att_banks = {}
+
+        def att_matmul(i):
+            att_banks[i] = [bank(2), bank(3)]
+            for hf in range(2):
+                for g in range(2):
+                    nc.tensor.matmul_mx(
+                        out=att_banks[i][hf][:],
+                        lhsT=v_codes[i][:, P * g : P * g + P].bitcast(FP8X4),
+                        lhsT_scale=v_scales[i][:, P * g : P * g + P],
+                        rhs=wo_codes[:, g, hf, :].bitcast(FP8X4),
+                        rhs_scale=wo_scales[:, g, hf, :],
+                        start=(g == 0),
+                        stop=(g == 1),
+                    )
+
+        lb, hb = {}, {}
+
+        def make_lb(i):
+            lb[i] = work.tile([P, H], F32, name="lb", tag="lb", bufs=2)
+            for hf in range(2):
+                s = slice(512 * hf, 512 * hf + 512)
+                nc.gpsimd.tensor_tensor(out=lb[i][:, s], in0=liq_sb[:, i, s], in1=bo_bc[:, s], op=ALU.add)
+
+        def make_hb(i):
+            hb[i] = work.tile([P, H], F32, name="hb", tag="hb", bufs=2)
+            for hf in range(2):
+                s = slice(512 * hf, 512 * hf + 512)
+                nc.gpsimd.tensor_tensor(out=hb[i][:, s], in0=h_raw[i][:, s], in1=om_bc[:, s], op=ALU.mult)
+
+        u, sums, negm, sq, rstd, nmr, nrm, y = {}, {}, {}, {}, {}, {}, {}, {}
+
+        def add_u(i):
+            u[i] = work.tile([P, H], F32, name="u", tag="u", bufs=3)
+            sums[i] = work.tile([P, 2], F32, name="sums", tag="sums", bufs=3)
+            negm[i] = work.tile([P, 1], F32, name="negm", tag="negm", bufs=4)
+            for hf in range(2):
+                s = slice(512 * hf, 512 * hf + 512)
+                nc.vector.scalar_tensor_tensor(
+                    out=u[i][:, s],
+                    in0=att_banks[i][hf][:],
+                    scalar=1.0,
+                    in1=lb[i][:, s],
+                    op0=ALU.mult,
+                    op1=ALU.add,
+                    accum_out=sums[i][:, hf : hf + 1],
+                )
+            nc.vector.tensor_scalar(
+                out=negm[i][:],
+                in0=sums[i][:, 0:1],
+                scalar1=sums[i][:, 1:2],
+                scalar2=-1.0 / H,
+                op0=ALU.add,
+                op1=ALU.mult,
+            )
+
+        def square(i):
+            sq[i] = work.tile([P, 1], F32, name="sq", tag="sq", bufs=3)
+            nrm[i] = work.tile([P, H], F32, name="nrm", tag="nrm", bufs=2)
+            nc.scalar.activation(
+                out=nrm[i][:], in_=u[i][:], func=ACT.Square, bias=negm[i][:], scale=1.0, accum_out=sq[i][:]
+            )
+
+        def stats(i):
+            rstd[i] = work.tile([P, 1], F32, name="rstd", tag="rstd", bufs=3)
+            nmr[i] = work.tile([P, 1], F32, name="nmr", tag="nmr", bufs=3)
+            varp = work.tile([P, 1], F32, name="varp", tag="varp", bufs=3)
+            nc.gpsimd.tensor_scalar(
+                out=varp[:], in0=sq[i][:], scalar1=1.0 / H, scalar2=LN_EPS, op0=ALU.mult, op1=ALU.add
+            )
+            nc.gpsimd.tensor_tensor(out=rstd[i][:], in0=varp[:], in1=half_neg[:], op=ALU.pow)
+            nc.gpsimd.tensor_tensor(out=nmr[i][:], in0=negm[i][:], in1=rstd[i][:], op=ALU.mult)
+
+        def normalise(i, hf):
+            s = slice(512 * hf, 512 * hf + 512)
+            nc.scalar.activation(
+                out=nrm[i][:, s], in_=u[i][:, s], func=ACT.Identity, bias=nmr[i][:], scale=rstd[i][:]
+            )
+
+        n_banks = {}
+
+        def turn_n(i, hf):
+            b = bank(4 + hf)
+            n_banks[i, hf] = b
+            for j in range(4):
+                nc.tensor.transpose(
+                    b[:, P * j : P * j + P], nrm[i][:, 512 * hf + P * j : 512 * hf + P * j + P], ident[:]
+                )
+
+        def gain(i, hf):
+            y[i, hf] = work.tile([P, 4, P], F32, name="y", tag="y", bufs=4)
+            for j in range(4):
+                jj = 4 * hf + j
+                nc.vector.scalar_tensor_tensor(
+                    out=y[i, hf][:, j, :],
+                    in0=n_banks[i, hf][:, P * j : P * j + P],
+                    scalar=cols[:, 16 + jj : 17 + jj],
+                    in1=xs[:, i // 4, jj, P * (i % 4) : P * (i % 4) + P],
+                    op0=ALU.mult,
+                    op1=ALU.add,
+                )
+
+        def tanh(i, hf):
+            flat = y[i, hf][:].rearrange("p j r -> p (j r)")
+            nc.scalar.activation(out=flat, in_=flat, func=ACT.Tanh)
+
+        def scale_w(i, hf):
+            if WROUTE[2 * i + hf] == "p":
+                return
+            for j in range(4):
+                jj = 4 * hf + j
+                if WROUTE[2 * i + hf] == "g":
+                    nc.gpsimd.tensor_scalar(
+                        out=y[i, hf][:, j, :], in0=y[i, hf][:, j, :], scalar1=it_col[:, jj : jj + 1], scalar2=0.0,
+                        op0=ALU.mult, op1=ALU.add,
+                    )
+                    continue
+                nc.scalar.activation(
+                    out=y[i, hf][:, j, :], in_=y[i, hf][:, j, :], func=ACT.Copy, scale=it_col[:, jj : jj + 1]
+                )
+
+        w_banks = {}
+
+        def turn_w(i, hf):
+            b = bank(6 + hf)
+            w_banks[i, hf] = b
+            for j in range(4):
+                if WROUTE[2 * i + hf] == "p":
+                    nc.tensor.matmul(b[:, P * j : P * j + P], lhsT=y[i, hf][:, j, :], rhs=diag[:, 4 * hf + j, :], start=True, stop=True)
+                else:
+                    nc.tensor.transpose(b[:, P * j : P * j + P], y[i, hf][:, j, :], ident[:])
+
+        def finish(i, hf):
+            s = slice(512 * hf, 512 * hf + 512)
+            o = work.tile([P, 512], F32, name="o", tag="o", bufs=3)
+            nc.vector.tensor_tensor(out=o[:], in0=w_banks[i, hf][:], in1=hb[i][:, s], op=ALU.add)
+            nc.sync.dma_start(out=out_view[i][:, s], in_=o[:])
+
+        def om_spread():
+            spread(om_bc, om_col, ident)
+            if "p" in WROUTE:
+                make_diag()
+
+        def item(name):
+            engine = "v" if "V" in name else "s"
+            if name == "par":
+                params()
+            elif name == "bo":
+                spread(bo_bc, bo_col, ident_bf)
+            elif name == "om":
+                om_spread()
+            elif name[0] == "w":
+                prep_wo(int(name[1]))
+            elif name[0] == "v":
+                prep_wv(int(name[1]), engine)
+            elif name[0] == "l":
+                prep_liq(int(name[1]), engine)
+            elif name[0] == "p":
+                prep_pair(int(name[1]), engine)
+            else:
+                xin(2 * int(name[1]), int(name[2]), engine)
+                xin(2 * int(name[1]) + 1, int(name[2]), engine)
+
+        def tanh_w(i, hf):
+            tanh(i, hf)
+            scale_w(i, hf)
+
+        token = {
+            "VM": v_matmul, "VE": v_evac, "VQ": v_quant, "AM": att_matmul, "A": add_u, "SQ": square, "ST": stats,
+            "N": normalise, "NT": turn_n, "G": gain, "T": tanh_w, "WT": turn_w, "F": finish, "LB": make_lb, "HB": make_hb,
+        }
+        cast_wo(0)
+        cast_wo(1)
+        for s in range(22):
+            if s < 6:
+                cast_wo(s + 2)
+            if s < len(SLOTS):
+                for name in SLOTS[s]:
+                    item(name)
+                    flush_q(1)
+            if s == 8:
+                flush_q(0)
+                for i in range(8):
+                    load_h(i)
+            k = s - 9
+            if k >= 0:
+                rotation["order"] = [6, 7]
+                for name, lag, part in STEP:
+                    if name == "LQ":
+                        flush_q(0)
+                    elif 0 <= k - lag < 8:
+                        if part is None:
+                            token[name](k - lag)
+                        else:
+                            token[name](k - lag, part)

@@ -18,11 +18,11 @@ ALU = mybir.AluOpType
 ACT = mybir.ActivationFunctionType
 
 LN_EPS = 1e-5
-CAST = "GGGGGGGG"
+CAST = "SSSSSSSS"
 WROUTE = ["s","p","s","p","s","p","s","p","s","p","s","p","s","p","s","p"]
-SLOTS = [["par","bo","p0","v4","w0"],["p1","w1"],["p5","p3","p7","w2"],["p4","v1","v2","l4","w3"],["v6","p2","l1","p6","w4"],["l0","om","w5"],["x30","v7","w6"],["v5","v0","w7","v3","l2"],["x21","x20V"],["x31","x01"],["l3","x11"],["x10"],["x00"],["l6","l5","l7"]]
-STEP = [["NT",4,1],["G",4,1],["LQ",0,None],["LB",0,None],["VM",0,None],["N",3,0],["T",5,1],["SQ",2,None],["T",4,0],["ST",2,None],["HB",4,None],["F",5,0],["N",3,1],["AM",1,None],["VE",0,None],["A",1,None],["NT",3,0],["VQ",0,None],["G",3,0],["WT",5,1],["F",5,1],["WT",4,0]]
-LOADS = ["o0","p0","v4","p1","o1","p5","p3","p7","p4","v1","v2","l4","o2","v6","p2","l1","p6","l0","o3","v7","v5","v0","v3","l2","l3","l6","l5","l7"]
+SLOTS = [["l7V","w0"],["w1","v3","p7"],["p4","v7","par","v1V","w2"],["w3"],["v2","v4V","bo","w4"],["l3","w5","om"],["w6","p0","v5","p5","p3","p1V","p6"],["l0","v6","v0","w7"],["x30","l1"],["l6","x31","x11"],["l2","p2"],["x21"],["x00","l5V","l4V"],["x20","x10V"],["x01"]]
+STEP = [["LQ",0,None],["NT",4,0],["G",4,0],["VM",0,None],["N",3,1],["G",4,1],["VE",0,None],["AM",1,None],["A",1,None],["WT",5,0],["SQ",2,None],["LB",0,None],["WT",5,1],["N",3,0],["F",5,0],["NT",3,1],["ST",2,None],["VQ",0,None],["T",4,0],["T",4,1],["HB",4,None],["F",5,1]]
+LOADS = ["o0","l7","v3","p7","o1","p4","v7","v1","o2","v2","v4","l3","o3","p0","v5","p5","p3","p1","p6","l0","v6","v0","l1","l6","l2","p2","l5","l4"]
 TAU_EPS = 1e-6
 
 
@@ -339,14 +339,14 @@ def tile_advancedliquidneuralnetwork_pb_kernel(
 
         def make_lb(i):
             lb[i] = work.tile([P, H], F32, name="lb", tag="lb", bufs=2)
-            for hf in range(2):
-                s = slice(512 * hf, 512 * hf + 512)
+            for quarter in range(4):
+                s = slice(256 * quarter, 256 * quarter + 256)
                 nc.gpsimd.tensor_tensor(out=lb[i][:, s], in0=liq_sb[:, i, s], in1=bo_bc[:, s], op=ALU.add)
 
         def make_hb(i):
             hb[i] = work.tile([P, H], F32, name="hb", tag="hb", bufs=2)
-            for hf in range(2):
-                s = slice(512 * hf, 512 * hf + 512)
+            for quarter in range(4):
+                s = slice(256 * quarter, 256 * quarter + 256)
                 nc.gpsimd.tensor_tensor(out=hb[i][:, s], in0=h_raw[i][:, s], in1=om_bc[:, s], op=ALU.mult)
 
         u, sums, negm, sq, rstd, nmr, nrm, y = {}, {}, {}, {}, {}, {}, {}, {}
@@ -498,7 +498,7 @@ def tile_advancedliquidneuralnetwork_pb_kernel(
             if s < len(SLOTS):
                 for name in SLOTS[s]:
                     item(name)
-                    flush_q(1)
+                    flush_q(2)
             if s == 8:
                 flush_q(0)
                 for i in range(8):

@@ -18,11 +18,13 @@ ALU = mybir.AluOpType
 ACT = mybir.ActivationFunctionType
 
 LN_EPS = 1e-5
-CAST = "SSSSSSSS"
-WROUTE = ["s","p","s","p","s","p","s","p","s","p","s","p","s","p","s","p"]
-SLOTS = [["l7V","w0"],["w1","v3","p7"],["p4","v7","par","v1V","w2"],["w3"],["v2","v4V","bo","w4"],["l3","w5","om"],["w6","p0","v5","p5","p3","p1V","p6"],["l0","v6","v0","w7"],["x30","l1"],["l6","x31","x11"],["l2","p2"],["x21"],["x00","l5V","l4V"],["x20","x10V"],["x01"]]
-STEP = [["LQ",0,None],["NT",4,0],["G",4,0],["VM",0,None],["N",3,1],["G",4,1],["VE",0,None],["AM",1,None],["A",1,None],["WT",5,0],["SQ",2,None],["LB",0,None],["WT",5,1],["N",3,0],["F",5,0],["NT",3,1],["ST",2,None],["VQ",0,None],["T",4,0],["T",4,1],["HB",4,None],["F",5,1]]
-LOADS = ["o0","l7","v3","p7","o1","p4","v7","v1","o2","v2","v4","l3","o3","p0","v5","p5","p3","p1","p6","l0","v6","v0","l1","l6","l2","p2","l5","l4"]
+CAST = "SSGSGSGS"
+LBP = 0
+NG = "SSSSSGSS"
+WROUTE = "spsqpppssppspsps"
+SLOTS = [["d0","v1M","l0","par","w0"],["w1"],["p0","p2","w2"],["w3","l3V","v0"],["l2","w4","v2"],["p1","w5"],["l1M","p3","bo","w6","v3","x00"],["w7","d3","x10M","x21M","x11M","x20"],[],["om"],["x31"],["x01"],["x30M"]]
+STEP = [["VQ",2,None],["NT",5,0],["F",7,1],["NT",5,1],["SQ",3,None],["N",4,0],["HB",6,None],["LB",0,None],["G",5,0],["N",4,1],["LQ",0,None],["T",5,0],["VM",1,None],["ST",3,None],["AM",2,None],["WT",6,0],["G",5,1],["VE",1,None],["A",2,None],["WT",6,1],["F",6,0],["T",5,1]]
+LOADS = ["o0","v1","l0","o1","p0","p2","l3","v0","o2","l2","v2","p1","o3","l1","p3","v3"]
 TAU_EPS = 1e-6
 
 
@@ -48,7 +50,7 @@ def tile_advancedliquidneuralnetwork_pb_kernel(
         om_col = keep.tile([P, 8], F32, name="om_col")
         bv_col = keep.tile([P, 2, 4], BF16, name="bv_col")
         sc_col = keep.tile([P, 2, 2, 2], F32, name="sc_col")
-        bo_bc = keep.tile([P, H], F32, name="bo_bc")
+        bo_bc = keep.tile([P, H], BF16, name="bo_bc")
         om_bc = keep.tile([P, H], F32, name="om_bc")
         half_neg = keep.tile([P, 1], F32, name="half_neg")
         ident_bf = keep.tile([P, P], BF16, name="ident_bf")
@@ -57,8 +59,8 @@ def tile_advancedliquidneuralnetwork_pb_kernel(
         warm = keep.tile([P, 1], F32, name="warm")
 
         liq_sb = keep.tile([P, 8, H], BF16, name="liq_sb", align_bytes=64)
-        x_sb = keep.tile([P, 4, 2, IN], BF16, name="x_sb", align_bytes=64)
-        win_sb = keep.tile([P, 4, 2, IN], BF16, name="win_sb", align_bytes=64)
+        x_sb = keep.tile([P, 8, IN], BF16, name="x_sb", align_bytes=64)
+        win_sb = keep.tile([P, 8, IN], BF16, name="win_sb", align_bytes=64)
         wo_sb = keep.tile([P, 8, H], U8, name="wo_sb", align_bytes=64)
 
         wv_codes = keep.tile([P, 8, 256], U32, name="wv_codes", align_bytes=64)
@@ -67,55 +69,68 @@ def tile_advancedliquidneuralnetwork_pb_kernel(
         liq_scales = keep.tile([P, 8, 256], U8, name="liq_scales", align_bytes=64)
         win_codes = keep.tile([P, 4, 256], U32, name="win_codes", align_bytes=64)
         win_scales = keep.tile([P, 4, 256], U8, name="win_scales", align_bytes=64)
-        x_codes = keep.tile([P, 2, 512], U32, name="x_codes", align_bytes=64)
-        x_scales = keep.tile([P, 2, 512], U8, name="x_scales", align_bytes=64)
+        x_codes = keep.tile([P, 4, 256], U32, name="x_codes", align_bytes=64)
+        x_scales = keep.tile([P, 4, 256], U8, name="x_scales", align_bytes=64)
         wo_codes = keep.tile([P, 2, 2, 512], U32, name="wo_codes", align_bytes=64)
         wo_scales = keep.tile([P, 2, 2, 512], U8, name="wo_scales", align_bytes=64)
         xs = keep.tile([P, 2, 8, 512], F32, name="xs")
 
         wv_raw = {}
         h_raw = {}
-        wv_view = W_v.rearrange("(g m t) k -> g t m k", m=P, t=4)
-        x_view = x.rearrange("(q a p) k -> q p a k", a=2, p=P)
-        win_view = W_in.rearrange("(q a p) k -> q p a k", a=2, p=P)
+        wv_view = W_v.rearrange("(g m s z) k -> g s m z k", m=P, s=2, z=2)
+        x_view = x.rearrange("(p h i) k -> h p i k", h=2, i=4)
+        win_view = W_in.rearrange("(h i p) k -> h p i k", h=2, p=P)
         wo_view = W_o_bytes.rearrange("(q a p) k -> q p a k", a=2, p=P)
-        liq_view = liq.rearrange("(i p) k -> i p k", p=P)
-        h_view = h.rearrange("(i p) k -> i p k", p=P)
-        out_view = out.rearrange("(i p) k -> i p k", p=P)
+        liq_view = liq.rearrange("(p i) k -> p i k", i=8)
+        h_view = h.rearrange("(p i) k -> p i k", i=8)
+        out_view = out.rearrange("(p i) k -> p i k", i=8)
 
-        def load_wv(c):
-            wv_raw[c] = work.tile([P, H], BF16, name="wv_raw", tag="raw", bufs=8, align_bytes=64)
-            nc.sync.dma_start(out=wv_raw[c][:], in_=wv_view[c // 4, c % 4])
+        def load(dst, src, parts):
+            step = dst.shape[1] // parts
+            for n in range(parts):
+                nc.sync.dma_start(out=dst[:, n * step : n * step + step], in_=src[:, n * step : n * step + step])
 
-        def load_h(i):
-            h_raw[i] = work.tile([P, H], BF16, name="h_raw", tag="raw", bufs=8, align_bytes=64)
-            nc.sync.dma_start(out=h_raw[i][:], in_=h_view[i])
+        def load_wv(n, parts):
+            wv_raw[n] = work.tile([P, 2, H], BF16, name="wv_raw", tag="raw", bufs=4, align_bytes=64)
+            load(wv_raw[n][:], wv_view[n // 2, n % 2], parts)
 
-        def load_liq(i):
-            nc.sync.dma_start(out=liq_sb[:, i, :], in_=liq_view[i])
+        def load_h(n):
+            h_raw[n] = work.tile([P, 2, H], BF16, name="h_raw", tag="raw", bufs=4, align_bytes=64)
+            load(h_raw[n][:], h_view[:, 2 * n : 2 * n + 2, :], 1)
+
+        def load_liq(n, parts):
+            load(liq_sb[:, 2 * n : 2 * n + 2, :], liq_view[:, 2 * n : 2 * n + 2, :], parts)
+
+        def load_double_x(n, parts):
+            if n < 2:
+                load(win_sb[:, 4 * n : 4 * n + 4], win_view[n], parts)
+            else:
+                load(x_sb[:, 4 * n - 8 : 4 * n - 4], x_view[n - 2], parts)
 
         def load_wo(q):
             nc.sync.dma_start(out=wo_sb[:, 2 * q : 2 * q + 2, :], in_=wo_view[q])
 
-        def load_pair(e):
-            if e < 4:
-                nc.sync.dma_start(out=win_sb[:, e], in_=win_view[e])
-            else:
-                nc.sync.dma_start(out=x_sb[:, e - 4], in_=x_view[e - 4])
 
         nc.vector.memset(rows[:], 0.0)
         nc.vector.memset(half_neg[:], -0.5)
         nc.vector.memset(warm[:], 0.0)
         make_identity(nc, ident[:])
-        nc.scalar.dma_start(out=sc_col[:], in_=W_o_scale.rearrange("o (g p u e) -> p (o g) u e", g=2, p=P, u=2))
-        nc.scalar.dma_start(out=bv_col[:], in_=b_v.rearrange("(g p t) -> p g t", g=2, p=P))
-        for n, vec in enumerate((b_in, beta_att, g_att, tau, b_o)):
-            nc.scalar.dma_start(out=rows[8 * n : 8 * n + 8, :], in_=vec.rearrange("(j p) -> j p", p=P))
         nc.scalar.activation(out=warm[:], in_=warm[:], func=ACT.Tanh)
 
-        loaders = {"o": load_wo, "v": load_wv, "l": load_liq, "p": load_pair}
-        for name in LOADS:
-            loaders[name[0]](int(name[1]))
+        def load_params():
+            nc.sync.dma_start(out=sc_col[:], in_=W_o_scale.rearrange("o (g p u e) -> p (o g) u e", g=2, p=P, u=2))
+            nc.sync.dma_start(out=bv_col[:], in_=b_v.rearrange("(g p t) -> p g t", g=2, p=P))
+            for n, vec in enumerate((b_in, beta_att, g_att, tau, b_o)):
+                nc.sync.dma_start(out=rows[8 * n : 8 * n + 8, :], in_=vec.rearrange("(j p) -> j p", p=P))
+
+        loaders = {"v": load_wv, "l": load_liq, "p": load_double_x}
+        for n, name in enumerate(LOADS):
+            if name[0] == "o":
+                load_wo(int(name[1]))
+            else:
+                loaders[name[0]](int(name[1]), 2 if n < 3 else 1)
+            if n == 2:
+                load_params()
 
         rotation = {"order": [2, 3, 4, 5, 6, 7], "at": 0}
 
@@ -151,48 +166,35 @@ def tile_advancedliquidneuralnetwork_pb_kernel(
         def quantize(codes, scales, src):
             nc.vector.quantize_mx(out=codes.bitcast(FP8X4), scales=scales, in_=src)
 
-        def prep_wv(c, engine):
-            b = next_bank()
-            word_transposes(b, words_of(wv_raw[c][:]))
-            gt = work.tile([P, 1024], BF16, name="grouped", tag="grouped", bufs=4, align_bytes=64)
-            copy_out(engine, gt[:], b)
-            pending_q.append(lambda: quantize(wv_codes[:, c, :], wv_scales[:, c, :], gt[:]))
-
-        def prep_liq(i, engine):
-            b = next_bank()
-            word_transposes(b, words_of(liq_sb[:, i, :]))
-            gt = work.tile([P, 1024], BF16, name="grouped", tag="grouped", bufs=4, align_bytes=64)
-            copy_out(engine, gt[:], b)
-            pending_q.append(lambda: quantize(liq_codes[:, i, :], liq_scales[:, i, :], gt[:]))
-
-        x_grouped = {}
-        x_done = []
-
-        def prep_pair(e, engine):
-            b = next_bank()
-            if e < 4:
-                words = [
-                    win_sb[:, e, a, :].bitcast(F32)[:, u:256:2] for a in range(2) for u in range(2)
-                ]
-                gt = work.tile([P, 1024], BF16, name="grouped", tag="grouped", bufs=4, align_bytes=64)
+        def prep_double(kind, n, engines):
+            gt = work.tile([P, 2, 1024], BF16, name="grouped", tag="grouped", bufs=3, align_bytes=64)
+            for z in range(2):
+                m = 2 * n + z
+                if kind == "v":
+                    words = words_of(wv_raw[n][:, z, :])
+                elif kind == "l":
+                    words = words_of(liq_sb[:, m, :])
+                else:
+                    rows_sb = win_sb[:, 2 * m : 2 * m + 2] if n < 2 else x_sb[:, 2 * m - 8 : 2 * m - 6]
+                    words = [rows_sb[:, a, :].bitcast(F32)[:, t:256:2] for a in range(2) for t in range(2)]
+                b = next_bank()
                 word_transposes(b, words)
-                copy_out(engine, gt[:], b)
-                pending_q.append(lambda: quantize(win_codes[:, e, :], win_scales[:, e, :], gt[:]))
+                copy_out(engines[z], gt[:, z], b)
+            if kind == "v":
+                codes, scales = wv_codes[:, 2 * n : 2 * n + 2, :], wv_scales[:, 2 * n : 2 * n + 2, :]
+            elif kind == "l":
+                codes, scales = liq_codes[:, 2 * n : 2 * n + 2, :], liq_scales[:, 2 * n : 2 * n + 2, :]
+            elif n < 2:
+                codes, scales = win_codes[:, 2 * n : 2 * n + 2, :], win_scales[:, 2 * n : 2 * n + 2, :]
             else:
-                q = e - 4
-                words = [
-                    x_sb[:, q, a, :].bitcast(F32)[:, u:256:2] for a in range(2) for u in range(2)
-                ]
-                if q // 2 not in x_grouped:
-                    x_grouped[q // 2] = work.tile(
-                        [P, 2048], BF16, name="x_grouped", tag="x_grouped", bufs=2, align_bytes=64
-                    )
-                gt = x_grouped[q // 2]
-                word_transposes(b, words)
-                copy_out(engine, gt[:, 1024 * (q % 2) : 1024 * (q % 2) + 1024], b)
-                x_done.append(q)
-                if q ^ 1 in x_done:
-                    pending_q.append(lambda: quantize(x_codes[:, q // 2, :], x_scales[:, q // 2, :], gt[:]))
+                codes, scales = x_codes[:, 2 * n - 4 : 2 * n - 2, :], x_scales[:, 2 * n - 4 : 2 * n - 2, :]
+            pending_q.append(
+                lambda: quantize(
+                    codes.rearrange("p a w -> p (a w)"),
+                    scales.rearrange("p a w -> p (a w)"),
+                    gt[:].rearrange("p z k -> p (z k)"),
+                )
+            )
 
         wo_bf = {}
         wo_grouped = {}
@@ -225,14 +227,13 @@ def tile_advancedliquidneuralnetwork_pb_kernel(
                     op=ALU.mult,
                 )
             if j == 3:
-                for g in range(2):
-                    pending_q.append(
-                        lambda g=g: quantize(
-                            wo_codes[:, g, hf, :],
-                            wo_scales[:, g, hf, :],
-                            gt[:, g].rearrange("p r t -> p (r t)"),
-                        )
+                pending_q.append(
+                    lambda: quantize(
+                        wo_codes[:, hf].rearrange("p g w -> p (g w)"),
+                        wo_scales[:, hf].rearrange("p g w -> p (g w)"),
+                        gt[:].rearrange("p g r t -> p (g r t)"),
                     )
+                )
 
         def params():
             nc.vector.tensor_copy(out=rows_f[:], in_=rows[:])
@@ -275,8 +276,8 @@ def tile_advancedliquidneuralnetwork_pb_kernel(
                 out=b[:],
                 lhsT=win_codes[:, j // 2, P * (j % 2) : P * (j % 2) + P].bitcast(FP8X4),
                 lhsT_scale=win_scales[:, j // 2, P * (j % 2) : P * (j % 2) + P],
-                rhs=x_codes[:, hf, :].bitcast(FP8X4),
-                rhs_scale=x_scales[:, hf, :],
+                rhs=x_codes[:, 2 * hf : 2 * hf + 2, :].rearrange("p a w -> p (a w)").bitcast(FP8X4),
+                rhs_scale=x_scales[:, 2 * hf : 2 * hf + 2, :].rearrange("p a w -> p (a w)"),
                 start=True,
                 stop=True,
             )
@@ -286,6 +287,11 @@ def tile_advancedliquidneuralnetwork_pb_kernel(
                 )
             else:
                 nc.scalar.activation(out=xs[:, hf, j, :], in_=b[:], func=ACT.Identity, bias=c_col[:, j : j + 1])
+
+        def keep_warm():
+            b = bank(1)
+            for n in range(2):
+                nc.tensor.matmul(b[:, 0:P], lhsT=ident[:], rhs=ident[:], start=True, stop=True)
 
         v_banks, v_grouped, v_codes, v_scales = {}, {}, {}, {}
 
@@ -329,27 +335,37 @@ def tile_advancedliquidneuralnetwork_pb_kernel(
                         out=att_banks[i][hf][:],
                         lhsT=v_codes[i][:, P * g : P * g + P].bitcast(FP8X4),
                         lhsT_scale=v_scales[i][:, P * g : P * g + P],
-                        rhs=wo_codes[:, g, hf, :].bitcast(FP8X4),
-                        rhs_scale=wo_scales[:, g, hf, :],
+                        rhs=wo_codes[:, hf, g, :].bitcast(FP8X4),
+                        rhs_scale=wo_scales[:, hf, g, :],
                         start=(g == 0),
                         stop=(g == 1),
                     )
 
         lb, hb = {}, {}
 
+        def prep_lb(i, engines):
+            lb[i] = work.tile([P, H], F32, name="lb", tag="lb", bufs=3)
+            for hf in range(2):
+                s = slice(512 * hf, 512 * hf + 512)
+                b = next_bank()
+                nc.tensor.matmul(b[:], lhsT=ident_bf[:], rhs=liq_sb[:, i, s], start=True, stop=False)
+                nc.tensor.matmul(b[:], lhsT=ident_bf[:], rhs=bo_bc[:, s], start=False, stop=True)
+                if engines[hf] == "v":
+                    nc.vector.tensor_copy(out=lb[i][:, s], in_=b[:])
+                else:
+                    nc.scalar.copy(out=lb[i][:, s], in_=b[:])
+
         def make_lb(i):
-            lb[i] = work.tile([P, H], F32, name="lb", tag="lb", bufs=2)
-            for quarter in range(4):
-                s = slice(256 * quarter, 256 * quarter + 256)
-                nc.gpsimd.tensor_tensor(out=lb[i][:, s], in0=liq_sb[:, i, s], in1=bo_bc[:, s], op=ALU.add)
+            if i < LBP:
+                return
+            lb[i] = work.tile([P, H], F32, name="lb", tag="lb", bufs=3)
+            nc.gpsimd.tensor_tensor(out=lb[i][:], in0=liq_sb[:, i, :], in1=bo_bc[:], op=ALU.add)
 
         def make_hb(i):
             hb[i] = work.tile([P, H], F32, name="hb", tag="hb", bufs=2)
-            for quarter in range(4):
-                s = slice(256 * quarter, 256 * quarter + 256)
-                nc.gpsimd.tensor_tensor(out=hb[i][:, s], in0=h_raw[i][:, s], in1=om_bc[:, s], op=ALU.mult)
+            nc.gpsimd.tensor_tensor(out=hb[i][:], in0=h_raw[i // 2][:, i % 2, :], in1=om_bc[:], op=ALU.mult)
 
-        u, sums, negm, sq, rstd, nmr, nrm, y = {}, {}, {}, {}, {}, {}, {}, {}
+        u, sums, negm, sq, varp, rstd, nmr, nrm, y = {}, {}, {}, {}, {}, {}, {}, {}, {}
 
         def add_u(i):
             u[i] = work.tile([P, H], F32, name="u", tag="u", bufs=3)
@@ -381,19 +397,26 @@ def tile_advancedliquidneuralnetwork_pb_kernel(
             nc.scalar.activation(
                 out=nrm[i][:], in_=u[i][:], func=ACT.Square, bias=negm[i][:], scale=1.0, accum_out=sq[i][:]
             )
+            varp[i] = work.tile([P, 1], F32, name="varp", tag="varp", bufs=3)
+            nc.scalar.activation(out=varp[i][:], in_=sq[i][:], func=ACT.Copy, scale=1.0 / H, bias=LN_EPS)
 
         def stats(i):
             rstd[i] = work.tile([P, 1], F32, name="rstd", tag="rstd", bufs=3)
-            nmr[i] = work.tile([P, 1], F32, name="nmr", tag="nmr", bufs=3)
-            varp = work.tile([P, 1], F32, name="varp", tag="varp", bufs=3)
-            nc.gpsimd.tensor_scalar(
-                out=varp[:], in0=sq[i][:], scalar1=1.0 / H, scalar2=LN_EPS, op0=ALU.mult, op1=ALU.add
-            )
-            nc.gpsimd.tensor_tensor(out=rstd[i][:], in0=varp[:], in1=half_neg[:], op=ALU.pow)
-            nc.gpsimd.tensor_tensor(out=nmr[i][:], in0=negm[i][:], in1=rstd[i][:], op=ALU.mult)
+            nc.gpsimd.tensor_tensor(out=rstd[i][:], in0=varp[i][:], in1=half_neg[:], op=ALU.pow)
 
         def normalise(i, hf):
+            if i not in nmr:
+                nmr[i] = work.tile([P, 1], F32, name="nmr", tag="nmr", bufs=3)
+                if NG[i] == "G":
+                    nc.gpsimd.tensor_tensor(out=nmr[i][:], in0=negm[i][:], in1=rstd[i][:], op=ALU.mult)
+                else:
+                    nc.scalar.activation(out=nmr[i][:], in_=negm[i][:], func=ACT.Copy, scale=rstd[i][:])
             s = slice(512 * hf, 512 * hf + 512)
+            if NG[i] == "G":
+                nc.gpsimd.tensor_scalar(
+                    out=nrm[i][:, s], in0=u[i][:, s], scalar1=rstd[i][:], scalar2=nmr[i][:], op0=ALU.mult, op1=ALU.add
+                )
+                return
             nc.scalar.activation(
                 out=nrm[i][:, s], in_=u[i][:, s], func=ACT.Identity, bias=nmr[i][:], scale=rstd[i][:]
             )
@@ -426,7 +449,7 @@ def tile_advancedliquidneuralnetwork_pb_kernel(
             nc.scalar.activation(out=flat, in_=flat, func=ACT.Tanh)
 
         def scale_w(i, hf):
-            if WROUTE[2 * i + hf] == "p":
+            if WROUTE[2 * i + hf] != "s":
                 return
             for j in range(4):
                 jj = 4 * hf + j
@@ -445,6 +468,15 @@ def tile_advancedliquidneuralnetwork_pb_kernel(
         def turn_w(i, hf):
             b = bank(6 + hf)
             w_banks[i, hf] = b
+            if WROUTE[2 * i + hf] == "q":
+                nc.tensor.matmul(
+                    b[:], lhsT=ident[:], rhs=hb[i][:, 512 * hf : 512 * hf + 512], start=True, stop=False
+                )
+                for j in range(4):
+                    nc.tensor.matmul(
+                        b[:, P * j : P * j + P], lhsT=y[i, hf][:, j, :], rhs=diag[:, 4 * hf + j, :], start=False, stop=(j == 3)
+                    )
+                return
             for j in range(4):
                 if WROUTE[2 * i + hf] == "p":
                     nc.tensor.matmul(b[:, P * j : P * j + P], lhsT=y[i, hf][:, j, :], rhs=diag[:, 4 * hf + j, :], start=True, stop=True)
@@ -454,33 +486,35 @@ def tile_advancedliquidneuralnetwork_pb_kernel(
         def finish(i, hf):
             s = slice(512 * hf, 512 * hf + 512)
             o = work.tile([P, 512], F32, name="o", tag="o", bufs=3)
-            nc.vector.tensor_tensor(out=o[:], in0=w_banks[i, hf][:], in1=hb[i][:, s], op=ALU.add)
-            nc.sync.dma_start(out=out_view[i][:, s], in_=o[:])
+            if WROUTE[2 * i + hf] == "q":
+                nc.scalar.copy(out=o[:], in_=w_banks[i, hf][:])
+            else:
+                nc.vector.tensor_tensor(out=o[:], in0=w_banks[i, hf][:], in1=hb[i][:, s], op=ALU.add)
+            nc.sync.dma_start(out=out_view[:, i, s], in_=o[:])
 
         def om_spread():
             spread(om_bc, om_col, ident)
-            if "p" in WROUTE:
-                make_diag()
+            make_diag()
 
         def item(name):
-            engine = "v" if "V" in name else "s"
+            engines = {"V": "vv", "M": "sv"}.get(name[-1], "ss")
             if name == "par":
                 params()
             elif name == "bo":
                 spread(bo_bc, bo_col, ident_bf)
+            elif name[0] == "b":
+                prep_lb(int(name[1]), engines)
+            elif name[0] == "d":
+                keep_warm()
             elif name == "om":
                 om_spread()
             elif name[0] == "w":
                 prep_wo(int(name[1]))
-            elif name[0] == "v":
-                prep_wv(int(name[1]), engine)
-            elif name[0] == "l":
-                prep_liq(int(name[1]), engine)
-            elif name[0] == "p":
-                prep_pair(int(name[1]), engine)
+            elif name[0] in "vlp":
+                prep_double(name[0], int(name[1]), engines)
             else:
-                xin(2 * int(name[1]), int(name[2]), engine)
-                xin(2 * int(name[1]) + 1, int(name[2]), engine)
+                xin(2 * int(name[1]), int(name[2]), engines[0])
+                xin(2 * int(name[1]) + 1, int(name[2]), engines[0])
 
         def tanh_w(i, hf):
             tanh(i, hf)
@@ -498,12 +532,12 @@ def tile_advancedliquidneuralnetwork_pb_kernel(
             if s < len(SLOTS):
                 for name in SLOTS[s]:
                     item(name)
-                    flush_q(2)
+                    flush_q(1)
             if s == 8:
                 flush_q(0)
-                for i in range(8):
-                    load_h(i)
-            k = s - 9
+                for n in range(4):
+                    load_h(n)
+            k = s - 7
             if k >= 0:
                 rotation["order"] = [6, 7]
                 for name, lag, part in STEP:

from contextlib import ExitStack

import concourse.mybir as mybir
from concourse.masks import make_identity

B, IN, H = 1024, 512, 1024
P = 128
FLOPS = 2 * B * H * (IN + H + H)

F32 = mybir.dt.float32
BF16 = mybir.dt.bfloat16
U32 = mybir.dt.uint32
U8 = mybir.dt.uint8
FP8 = mybir.dt.float8_e4m3fn
FP8X4 = mybir.dt.float8_e4m3fn_x4

ALU = mybir.AluOpType
ACT = mybir.ActivationFunctionType

LN_EPS = 1e-5
CAST = "SSGSGSGS"
LBP = 0
NG = "SSSSSGSS"
WROUTE = "spsqpppssppspsps"
SLOTS = [["d0","v1M","l0","par","w0"],["w1"],["p0","p2","w2"],["w3","l3V","v0"],["l2","w4","v2"],["p1","w5"],["l1M","p3","bo","w6","v3","x00"],["w7","d3","x10M","x21M","x11M","x20"],[],["om"],["x31"],["x01"],["x30M"]]
STEP = [["VQ",2,None],["NT",5,0],["F",7,1],["NT",5,1],["SQ",3,None],["N",4,0],["HB",6,None],["LB",0,None],["G",5,0],["N",4,1],["LQ",0,None],["T",5,0],["VM",1,None],["ST",3,None],["AM",2,None],["WT",6,0],["G",5,1],["VE",1,None],["A",2,None],["WT",6,1],["F",6,0],["T",5,1]]
LOADS = ["o0","v1","l0","o1","p0","p2","l3","v0","o2","l2","v2","p1","o3","l1","p3","v3"]
TAU_EPS = 1e-6


def tile_advancedliquidneuralnetwork_pb_kernel(
    tc, liq, h, x, W_in, b_in, W_v, b_v, W_o_bytes, W_o_scale, b_o, g_att, beta_att, tau, out
):
    nc = tc.nc
    with ExitStack() as ctx:
        keep = ctx.enter_context(tc.tile_pool(name="keep", bufs=1))
        work = ctx.enter_context(tc.tile_pool(name="work", bufs=1))
        psum = ctx.enter_context(tc.psum_pool(name="psum", bufs=1))
        ctx.enter_context(tc.manual_schedule())

        def bank(n):
            return psum.tile([P, 512], F32, name="bank%d" % n, tag="bank%d" % n, bufs=1)

        ident = keep.tile([P, P], F32, name="ident")
        rows = keep.tile([P, P], BF16, name="rows")
        rows_f = keep.tile([P, P], F32, name="rows_f")
        cols = keep.tile([P, 40], F32, name="cols")
        c_col = keep.tile([P, 8], F32, name="c_col")
        it_col = keep.tile([P, 8], F32, name="it_col")
        om_col = keep.tile([P, 8], F32, name="om_col")
        bv_col = keep.tile([P, 2, 4], BF16, name="bv_col")
        sc_col = keep.tile([P, 2, 2, 2], F32, name="sc_col")
        bo_bc = keep.tile([P, H], BF16, name="bo_bc")
        om_bc = keep.tile([P, H], F32, name="om_bc")
        half_neg = keep.tile([P, 1], F32, name="half_neg")
        ident_bf = keep.tile([P, P], BF16, name="ident_bf")
        bo_col = keep.tile([P, 8], BF16, name="bo_col")
        diag = keep.tile([P, 8, P], F32, name="diag")
        warm = keep.tile([P, 1], F32, name="warm")

        liq_sb = keep.tile([P, 8, H], BF16, name="liq_sb", align_bytes=64)
        x_sb = keep.tile([P, 8, IN], BF16, name="x_sb", align_bytes=64)
        win_sb = keep.tile([P, 8, IN], BF16, name="win_sb", align_bytes=64)
        wo_sb = keep.tile([P, 8, H], U8, name="wo_sb", align_bytes=64)

        wv_codes = keep.tile([P, 8, 256], U32, name="wv_codes", align_bytes=64)
        wv_scales = keep.tile([P, 8, 256], U8, name="wv_scales", align_bytes=64)
        liq_codes = keep.tile([P, 8, 256], U32, name="liq_codes", align_bytes=64)
        liq_scales = keep.tile([P, 8, 256], U8, name="liq_scales", align_bytes=64)
        win_codes = keep.tile([P, 4, 256], U32, name="win_codes", align_bytes=64)
        win_scales = keep.tile([P, 4, 256], U8, name="win_scales", align_bytes=64)
        x_codes = keep.tile([P, 4, 256], U32, name="x_codes", align_bytes=64)
        x_scales = keep.tile([P, 4, 256], U8, name="x_scales", align_bytes=64)
        wo_codes = keep.tile([P, 2, 2, 512], U32, name="wo_codes", align_bytes=64)
        wo_scales = keep.tile([P, 2, 2, 512], U8, name="wo_scales", align_bytes=64)
        xs = keep.tile([P, 2, 8, 512], F32, name="xs")

        wv_raw = {}
        h_raw = {}
        wv_view = W_v.rearrange("(g m s z) k -> g s m z k", m=P, s=2, z=2)
        x_view = x.rearrange("(p h i) k -> h p i k", h=2, i=4)
        win_view = W_in.rearrange("(h i p) k -> h p i k", h=2, p=P)
        wo_view = W_o_bytes.rearrange("(q a p) k -> q p a k", a=2, p=P)
        liq_view = liq.rearrange("(p i) k -> p i k", i=8)
        h_view = h.rearrange("(p i) k -> p i k", i=8)
        out_view = out.rearrange("(p i) k -> p i k", i=8)

        def load(dst, src, parts):
            step = dst.shape[1] // parts
            for n in range(parts):
                nc.sync.dma_start(out=dst[:, n * step : n * step + step], in_=src[:, n * step : n * step + step])

        def load_wv(n, parts):
            wv_raw[n] = work.tile([P, 2, H], BF16, name="wv_raw", tag="raw", bufs=4, align_bytes=64)
            load(wv_raw[n][:], wv_view[n // 2, n % 2], parts)

        def load_h(n):
            h_raw[n] = work.tile([P, 2, H], BF16, name="h_raw", tag="raw", bufs=4, align_bytes=64)
            load(h_raw[n][:], h_view[:, 2 * n : 2 * n + 2, :], 1)

        def load_liq(n, parts):
            load(liq_sb[:, 2 * n : 2 * n + 2, :], liq_view[:, 2 * n : 2 * n + 2, :], parts)

        def load_double_x(n, parts):
            if n < 2:
                load(win_sb[:, 4 * n : 4 * n + 4], win_view[n], parts)
            else:
                load(x_sb[:, 4 * n - 8 : 4 * n - 4], x_view[n - 2], parts)

        def load_wo(q):
            nc.sync.dma_start(out=wo_sb[:, 2 * q : 2 * q + 2, :], in_=wo_view[q])


        nc.vector.memset(rows[:], 0.0)
        nc.vector.memset(half_neg[:], -0.5)
        nc.vector.memset(warm[:], 0.0)
        make_identity(nc, ident[:])
        nc.scalar.activation(out=warm[:], in_=warm[:], func=ACT.Tanh)

        def load_params():
            nc.sync.dma_start(out=sc_col[:], in_=W_o_scale.rearrange("o (g p u e) -> p (o g) u e", g=2, p=P, u=2))
            nc.sync.dma_start(out=bv_col[:], in_=b_v.rearrange("(g p t) -> p g t", g=2, p=P))
            for n, vec in enumerate((b_in, beta_att, g_att, tau, b_o)):
                nc.sync.dma_start(out=rows[8 * n : 8 * n + 8, :], in_=vec.rearrange("(j p) -> j p", p=P))

        loaders = {"v": load_wv, "l": load_liq, "p": load_double_x}
        for n, name in enumerate(LOADS):
            if name[0] == "o":
                load_wo(int(name[1]))
            else:
                loaders[name[0]](int(name[1]), 2 if n < 3 else 1)
            if n == 2:
                load_params()

        rotation = {"order": [2, 3, 4, 5, 6, 7], "at": 0}

        def next_bank():
            order = rotation["order"]
            b = bank(order[rotation["at"] % len(order)])
            rotation["at"] += 1
            return b

        pending_q = []

        def flush_q(keep_back):
            while len(pending_q) > keep_back:
                pending_q.pop(0)()

        def word_transposes(b, words):
            bv = b[:].rearrange("p (s r) -> p s r", s=4)
            for s, w in enumerate(words):
                nc.tensor.transpose(bv[:, s, :], w, ident[:])

        def words_of(tile_ap):
            w = tile_ap.bitcast(F32)
            return [w[:, 256 * g + u : 256 * (g + 1) : 2] for g in range(2) for u in range(2)]

        def copy_out(engine, dst_bf16, b):
            d = dst_bf16.bitcast(F32).rearrange("p (g r u) -> p g r u", g=2, u=2)
            s = b[:].rearrange("p (g u r) -> p g r u", g=2, u=2)
            if engine == "v":
                nc.vector.tensor_copy(out=d, in_=s)
            else:
                nc.scalar.copy(out=d, in_=s)

        def quantize(codes, scales, src):
            nc.vector.quantize_mx(out=codes.bitcast(FP8X4), scales=scales, in_=src)

        def prep_double(kind, n, engines):
            gt = work.tile([P, 2, 1024], BF16, name="grouped", tag="grouped", bufs=3, align_bytes=64)
            for z in range(2):
                m = 2 * n + z
                if kind == "v":
                    words = words_of(wv_raw[n][:, z, :])
                elif kind == "l":
                    words = words_of(liq_sb[:, m, :])
                else:
                    rows_sb = win_sb[:, 2 * m : 2 * m + 2] if n < 2 else x_sb[:, 2 * m - 8 : 2 * m - 6]
                    words = [rows_sb[:, a, :].bitcast(F32)[:, t:256:2] for a in range(2) for t in range(2)]
                b = next_bank()
                word_transposes(b, words)
                copy_out(engines[z], gt[:, z], b)
            if kind == "v":
                codes, scales = wv_codes[:, 2 * n : 2 * n + 2, :], wv_scales[:, 2 * n : 2 * n + 2, :]
            elif kind == "l":
                codes, scales = liq_codes[:, 2 * n : 2 * n + 2, :], liq_scales[:, 2 * n : 2 * n + 2, :]
            elif n < 2:
                codes, scales = win_codes[:, 2 * n : 2 * n + 2, :], win_scales[:, 2 * n : 2 * n + 2, :]
            else:
                codes, scales = x_codes[:, 2 * n - 4 : 2 * n - 2, :], x_scales[:, 2 * n - 4 : 2 * n - 2, :]
            pending_q.append(
                lambda: quantize(
                    codes.rearrange("p a w -> p (a w)"),
                    scales.rearrange("p a w -> p (a w)"),
                    gt[:].rearrange("p z k -> p (z k)"),
                )
            )

        wo_bf = {}
        wo_grouped = {}

        def cast_wo(c):
            wo_bf[c] = work.tile([P, H], BF16, name="wo_bf", tag="wo_bf", bufs=3, align_bytes=64)
            src = wo_sb[:, c, :].bitcast(FP8)
            if CAST[c] == "G":
                nc.gpsimd.tensor_copy(out=wo_bf[c][:], in_=src)
            elif CAST[c] == "V":
                nc.vector.tensor_copy(out=wo_bf[c][:], in_=src)
            else:
                nc.scalar.copy(out=wo_bf[c][:], in_=src)

        def prep_wo(c):
            b = next_bank()
            word_transposes(b, words_of(wo_bf[c][:]))
            hf, j = c // 4, c % 4
            if j == 0:
                wo_grouped[hf] = work.tile(
                    [P, 2, 512, 4], BF16, name="wo_grouped", tag="wo_grouped", bufs=2, align_bytes=64
                )
            gt = wo_grouped[hf]
            values = b[:].bitcast(BF16).rearrange("p (g u r e) -> p g r u e", g=2, u=2, e=2)
            for g in range(2):
                nc.vector.tensor_tensor(
                    out=gt[:, g, P * j : P * j + P, :].rearrange("p r (u e) -> p r u e", u=2),
                    in0=values[:, g],
                    in1=sc_col[:, g].unsqueeze(1).to_broadcast([P, P, 2, 2]),
                    op=ALU.mult,
                )
            if j == 3:
                pending_q.append(
                    lambda: quantize(
                        wo_codes[:, hf].rearrange("p g w -> p (g w)"),
                        wo_scales[:, hf].rearrange("p g w -> p (g w)"),
                        gt[:].rearrange("p g r t -> p (g r t)"),
                    )
                )

        def params():
            nc.vector.tensor_copy(out=rows_f[:], in_=rows[:])
            nc.vector.tensor_copy(out=ident_bf[:], in_=ident[:])
            b = next_bank()
            nc.tensor.transpose(b[:, 0:P], rows_f[:], ident[:])
            nc.vector.tensor_copy(out=cols[:], in_=b[:, 0:40])
            nc.vector.tensor_scalar(
                out=it_col[:], in0=cols[:, 24:32], scalar1=TAU_EPS, scalar2=None, op0=ALU.add
            )
            nc.vector.tensor_tensor(out=c_col[:], in0=cols[:, 0:8], in1=cols[:, 8:16], op=ALU.add)
            nc.vector.tensor_copy(out=bo_col[:], in_=cols[:, 32:40])
            nc.vector.reciprocal(out=it_col[:], in_=it_col[:])
            nc.vector.tensor_scalar(
                out=om_col[:], in0=it_col[:], scalar1=-1.0, scalar2=1.0, op0=ALU.mult, op1=ALU.add
            )

        def make_diag():
            for j in range(8):
                nc.gpsimd.tensor_scalar(
                    out=diag[:, j, :], in0=ident[:], scalar1=it_col[:, j : j + 1], scalar2=0.0, op0=ALU.mult, op1=ALU.add
                )

        def spread(dst, col, eye, halves=(0, 1)):
            for hf in halves:
                b = next_bank()
                for j in range(4):
                    nc.tensor.matmul(
                        b[:, P * j : P * j + P],
                        lhsT=col[:, 4 * hf + j : 4 * hf + j + 1].to_broadcast([P, P]),
                        rhs=eye[:],
                        start=True,
                        stop=True,
                    )
                nc.scalar.copy(out=dst[:, 512 * hf : 512 * hf + 512], in_=b[:])

        def xin(j, hf, engine):
            b = next_bank()
            nc.tensor.matmul_mx(
                out=b[:],
                lhsT=win_codes[:, j // 2, P * (j % 2) : P * (j % 2) + P].bitcast(FP8X4),
                lhsT_scale=win_scales[:, j // 2, P * (j % 2) : P * (j % 2) + P],
                rhs=x_codes[:, 2 * hf : 2 * hf + 2, :].rearrange("p a w -> p (a w)").bitcast(FP8X4),
                rhs_scale=x_scales[:, 2 * hf : 2 * hf + 2, :].rearrange("p a w -> p (a w)"),
                start=True,
                stop=True,
            )
            if engine == "v":
                nc.vector.tensor_scalar(
                    out=xs[:, hf, j, :], in0=b[:], scalar1=c_col[:, j : j + 1], scalar2=None, op0=ALU.add
                )
            else:
                nc.scalar.activation(out=xs[:, hf, j, :], in_=b[:], func=ACT.Identity, bias=c_col[:, j : j + 1])

        def keep_warm():
            b = bank(1)
            for n in range(2):
                nc.tensor.matmul(b[:, 0:P], lhsT=ident[:], rhs=ident[:], start=True, stop=True)

        v_banks, v_grouped, v_codes, v_scales = {}, {}, {}, {}

        def v_matmul(i):
            v_banks[i] = [bank(0), bank(1)]
            for go in range(2):
                for t in range(4):
                    for kg in range(2):
                        nc.tensor.matmul_mx(
                            out=v_banks[i][go][:, P * t : P * t + P],
                            lhsT=wv_codes[:, 4 * go + t, P * kg : P * kg + P].bitcast(FP8X4),
                            lhsT_scale=wv_scales[:, 4 * go + t, P * kg : P * kg + P],
                            rhs=liq_codes[:, i, P * kg : P * kg + P].bitcast(FP8X4),
                            rhs_scale=liq_scales[:, i, P * kg : P * kg + P],
                            start=(kg == 0),
                            stop=(kg == 1),
                        )

        def v_evac(i):
            v_grouped[i] = work.tile([P, 2, P, 4], BF16, name="v_grouped", tag="v_grouped", bufs=2, align_bytes=64)
            for go in range(2):
                nc.vector.tensor_tensor(
                    out=v_grouped[i][:, go],
                    in0=v_banks[i][go][:].rearrange("p (t n) -> p n t", t=4),
                    in1=bv_col[:, go].unsqueeze(1).to_broadcast([P, P, 4]),
                    op=ALU.add,
                )

        def v_quant(i):
            v_codes[i] = work.tile([P, 256], U32, name="v_codes", tag="v_codes", bufs=2, align_bytes=64)
            v_scales[i] = work.tile([P, 256], U8, name="v_scales", tag="v_scales", bufs=2, align_bytes=64)
            quantize(v_codes[i][:], v_scales[i][:], v_grouped[i][:].rearrange("p g n t -> p (g n t)"))

        att_banks = {}

        def att_matmul(i):
            att_banks[i] = [bank(2), bank(3)]
            for hf in range(2):
                for g in range(2):
                    nc.tensor.matmul_mx(
                        out=att_banks[i][hf][:],
                        lhsT=v_codes[i][:, P * g : P * g + P].bitcast(FP8X4),
                        lhsT_scale=v_scales[i][:, P * g : P * g + P],
                        rhs=wo_codes[:, hf, g, :].bitcast(FP8X4),
                        rhs_scale=wo_scales[:, hf, g, :],
                        start=(g == 0),
                        stop=(g == 1),
                    )

        lb, hb = {}, {}

        def prep_lb(i, engines):
            lb[i] = work.tile([P, H], F32, name="lb", tag="lb", bufs=3)
            for hf in range(2):
                s = slice(512 * hf, 512 * hf + 512)
                b = next_bank()
                nc.tensor.matmul(b[:], lhsT=ident_bf[:], rhs=liq_sb[:, i, s], start=True, stop=False)
                nc.tensor.matmul(b[:], lhsT=ident_bf[:], rhs=bo_bc[:, s], start=False, stop=True)
                if engines[hf] == "v":
                    nc.vector.tensor_copy(out=lb[i][:, s], in_=b[:])
                else:
                    nc.scalar.copy(out=lb[i][:, s], in_=b[:])

        def make_lb(i):
            if i < LBP:
                return
            lb[i] = work.tile([P, H], F32, name="lb", tag="lb", bufs=3)
            nc.gpsimd.tensor_tensor(out=lb[i][:], in0=liq_sb[:, i, :], in1=bo_bc[:], op=ALU.add)

        def make_hb(i):
            hb[i] = work.tile([P, H], F32, name="hb", tag="hb", bufs=2)
            nc.gpsimd.tensor_tensor(out=hb[i][:], in0=h_raw[i // 2][:, i % 2, :], in1=om_bc[:], op=ALU.mult)

        u, sums, negm, sq, varp, rstd, nmr, nrm, y = {}, {}, {}, {}, {}, {}, {}, {}, {}

        def add_u(i):
            u[i] = work.tile([P, H], F32, name="u", tag="u", bufs=3)
            sums[i] = work.tile([P, 2], F32, name="sums", tag="sums", bufs=3)
            negm[i] = work.tile([P, 1], F32, name="negm", tag="negm", bufs=4)
            for hf in range(2):
                s = slice(512 * hf, 512 * hf + 512)
                nc.vector.scalar_tensor_tensor(
                    out=u[i][:, s],
                    in0=att_banks[i][hf][:],
                    scalar=1.0,
                    in1=lb[i][:, s],
                    op0=ALU.mult,
                    op1=ALU.add,
                    accum_out=sums[i][:, hf : hf + 1],
                )
            nc.vector.tensor_scalar(
                out=negm[i][:],
                in0=sums[i][:, 0:1],
                scalar1=sums[i][:, 1:2],
                scalar2=-1.0 / H,
                op0=ALU.add,
                op1=ALU.mult,
            )

        def square(i):
            sq[i] = work.tile([P, 1], F32, name="sq", tag="sq", bufs=3)
            nrm[i] = work.tile([P, H], F32, name="nrm", tag="nrm", bufs=2)
            nc.scalar.activation(
                out=nrm[i][:], in_=u[i][:], func=ACT.Square, bias=negm[i][:], scale=1.0, accum_out=sq[i][:]
            )
            varp[i] = work.tile([P, 1], F32, name="varp", tag="varp", bufs=3)
            nc.scalar.activation(out=varp[i][:], in_=sq[i][:], func=ACT.Copy, scale=1.0 / H, bias=LN_EPS)

        def stats(i):
            rstd[i] = work.tile([P, 1], F32, name="rstd", tag="rstd", bufs=3)
            nc.gpsimd.tensor_tensor(out=rstd[i][:], in0=varp[i][:], in1=half_neg[:], op=ALU.pow)

        def normalise(i, hf):
            if i not in nmr:
                nmr[i] = work.tile([P, 1], F32, name="nmr", tag="nmr", bufs=3)
                if NG[i] == "G":
                    nc.gpsimd.tensor_tensor(out=nmr[i][:], in0=negm[i][:], in1=rstd[i][:], op=ALU.mult)
                else:
                    nc.scalar.activation(out=nmr[i][:], in_=negm[i][:], func=ACT.Copy, scale=rstd[i][:])
            s = slice(512 * hf, 512 * hf + 512)
            if NG[i] == "G":
                nc.gpsimd.tensor_scalar(
                    out=nrm[i][:, s], in0=u[i][:, s], scalar1=rstd[i][:], scalar2=nmr[i][:], op0=ALU.mult, op1=ALU.add
                )
                return
            nc.scalar.activation(
                out=nrm[i][:, s], in_=u[i][:, s], func=ACT.Identity, bias=nmr[i][:], scale=rstd[i][:]
            )

        n_banks = {}

        def turn_n(i, hf):
            b = bank(4 + hf)
            n_banks[i, hf] = b
            for j in range(4):
                nc.tensor.transpose(
                    b[:, P * j : P * j + P], nrm[i][:, 512 * hf + P * j : 512 * hf + P * j + P], ident[:]
                )

        def gain(i, hf):
            y[i, hf] = work.tile([P, 4, P], F32, name="y", tag="y", bufs=4)
            for j in range(4):
                jj = 4 * hf + j
                nc.vector.scalar_tensor_tensor(
                    out=y[i, hf][:, j, :],
                    in0=n_banks[i, hf][:, P * j : P * j + P],
                    scalar=cols[:, 16 + jj : 17 + jj],
                    in1=xs[:, i // 4, jj, P * (i % 4) : P * (i % 4) + P],
                    op0=ALU.mult,
                    op1=ALU.add,
                )

        def tanh(i, hf):
            flat = y[i, hf][:].rearrange("p j r -> p (j r)")
            nc.scalar.activation(out=flat, in_=flat, func=ACT.Tanh)

        def scale_w(i, hf):
            if WROUTE[2 * i + hf] != "s":
                return
            for j in range(4):
                jj = 4 * hf + j
                if WROUTE[2 * i + hf] == "g":
                    nc.gpsimd.tensor_scalar(
                        out=y[i, hf][:, j, :], in0=y[i, hf][:, j, :], scalar1=it_col[:, jj : jj + 1], scalar2=0.0,
                        op0=ALU.mult, op1=ALU.add,
                    )
                    continue
                nc.scalar.activation(
                    out=y[i, hf][:, j, :], in_=y[i, hf][:, j, :], func=ACT.Copy, scale=it_col[:, jj : jj + 1]
                )

        w_banks = {}

        def turn_w(i, hf):
            b = bank(6 + hf)
            w_banks[i, hf] = b
            if WROUTE[2 * i + hf] == "q":
                nc.tensor.matmul(
                    b[:], lhsT=ident[:], rhs=hb[i][:, 512 * hf : 512 * hf + 512], start=True, stop=False
                )
                for j in range(4):
                    nc.tensor.matmul(
                        b[:, P * j : P * j + P], lhsT=y[i, hf][:, j, :], rhs=diag[:, 4 * hf + j, :], start=False, stop=(j == 3)
                    )
                return
            for j in range(4):
                if WROUTE[2 * i + hf] == "p":
                    nc.tensor.matmul(b[:, P * j : P * j + P], lhsT=y[i, hf][:, j, :], rhs=diag[:, 4 * hf + j, :], start=True, stop=True)
                else:
                    nc.tensor.transpose(b[:, P * j : P * j + P], y[i, hf][:, j, :], ident[:])

        def finish(i, hf):
            s = slice(512 * hf, 512 * hf + 512)
            o = work.tile([P, 512], F32, name="o", tag="o", bufs=3)
            if WROUTE[2 * i + hf] == "q":
                nc.scalar.copy(out=o[:], in_=w_banks[i, hf][:])
            else:
                nc.vector.tensor_tensor(out=o[:], in0=w_banks[i, hf][:], in1=hb[i][:, s], op=ALU.add)
            nc.sync.dma_start(out=out_view[:, i, s], in_=o[:])

        def om_spread():
            spread(om_bc, om_col, ident)
            make_diag()

        def item(name):
            engines = {"V": "vv", "M": "sv"}.get(name[-1], "ss")
            if name == "par":
                params()
            elif name == "bo":
                spread(bo_bc, bo_col, ident_bf)
            elif name[0] == "b":
                prep_lb(int(name[1]), engines)
            elif name[0] == "d":
                keep_warm()
            elif name == "om":
                om_spread()
            elif name[0] == "w":
                prep_wo(int(name[1]))
            elif name[0] in "vlp":
                prep_double(name[0], int(name[1]), engines)
            else:
                xin(2 * int(name[1]), int(name[2]), engines[0])
                xin(2 * int(name[1]) + 1, int(name[2]), engines[0])

        def tanh_w(i, hf):
            tanh(i, hf)
            scale_w(i, hf)

        token = {
            "VM": v_matmul, "VE": v_evac, "VQ": v_quant, "AM": att_matmul, "A": add_u, "SQ": square, "ST": stats,
            "N": normalise, "NT": turn_n, "G": gain, "T": tanh_w, "WT": turn_w, "F": finish, "LB": make_lb, "HB": make_hb,
        }
        cast_wo(0)
        cast_wo(1)
        for s in range(22):
            if s < 6:
                cast_wo(s + 2)
            if s < len(SLOTS):
                for name in SLOTS[s]:
                    item(name)
                    flush_q(1)
            if s == 8:
                flush_q(0)
                for n in range(4):
                    load_h(n)
            k = s - 7
            if k >= 0:
                rotation["order"] = [6, 7]
                for name, lag, part in STEP:
                    if name == "LQ":
                        flush_q(0)
                    elif 0 <= k - lag < 8:
                        if part is None:
                            token[name](k - lag)
                        else:
                            token[name](k - lag, part)
